import numpy as np
import ml_dtypes


def mxq(x, axis, fmt="e4m3"):
    dtype, down = {"e4m3": (ml_dtypes.float8_e4m3fn, 7), "e5m2": (ml_dtypes.float8_e5m2, 14)}[fmt]
    v = np.moveaxis(np.asarray(x, np.float32).astype(ml_dtypes.bfloat16).astype(np.float64), axis, -1)
    blocks = v.reshape(v.shape[:-1] + (-1, 32))
    amax = np.abs(blocks).max(-1, keepdims=True)
    byte = np.maximum(np.where(amax > 0, np.frexp(amax)[1] - 1 + 127, 0) - down, 1)
    scale = np.exp2(byte - 127.0)
    codes = (blocks / scale).astype(np.float32).astype(dtype).astype(np.float64)
    return np.moveaxis((codes * scale).reshape(v.shape), -1, axis)


WIDE = False


def mx_kscale(k):
    if not WIDE:
        return np.ones(k)
    levels = np.array([10, -10, 5, -5, 0])
    if k % 512:
        return np.exp2(np.random.permutation(np.resize(levels, k // 32))).repeat(32)
    a = np.empty((k // 512, 16))
    for p in range(k // 512):
        a[p, :8] = np.random.permutation(np.resize(levels, 8))
        for g in range(8):
            far = levels[np.abs(levels - a[p, g]) >= 10]
            a[p, g + 8] = far[np.random.randint(len(far))]
    return np.exp2(a.ravel()).repeat(32)


BF16 = ml_dtypes.bfloat16


def bf(x):
    return np.asarray(x, np.float32).astype(BF16)


def f64(x):
    return np.asarray(x).astype(np.float64)


B, K, G, D, FF, F, P, H = 16, 64, 128, 1024, 2048, 2048, 7, 8
NC = K * G
EPS = 1e-5


def layernorm(x, g, b):
    m = x.mean(-1, keepdims=True)
    v = ((x - m) ** 2).mean(-1, keepdims=True)
    return (x - m) / np.sqrt(v + EPS) * g + b


def draw0():
    n = np.random.standard_normal
    s, t = mx_kscale(FF), mx_kscale(D)
    return {
        "ff_hid": bf(np.maximum(n((B, K, FF)), 0.0) * s),
        "tgt": bf(n((B, K, D))),
        "w2": bf(n((FF, D)) / np.sqrt(FF) / s[:, None]),
        "b2": bf(0.1 * n(D)),
        "g3": bf((1.0 + 0.1 * n(D)) * t),
        "be3": bf(0.1 * n(D) * t),
        "dup_pool": bf(n((K, D, G)) / np.sqrt(D) / t[None, :, None]),
        "dup_bias": bf(0.2 * n(NC)),
    }


def core(ff_hid, tgt, w2, b2, g3, be3, dup_pool, dup_bias):
    ff = (mxq(f64(ff_hid), 2, "e4m3") @ mxq(f64(w2), 0, "e4m3")) + f64(b2)
    h = layernorm(f64(tgt) + ff, f64(g3), f64(be3))
    out_extrap = (mxq(h, 2, "e4m3").transpose(1, 0, 2) @ mxq(f64(dup_pool), 1, "e4m3")).transpose(1, 0, 2)
    return out_extrap.reshape(B, -1)[:, :NC] + f64(dup_bias)


def e4m3fn_bytes(y):
    return np.clip(np.asarray(y, np.float64), -448.0, 448.0).astype(np.float32).astype(ml_dtypes.float8_e4m3fn).view(np.uint8)


def e4m3fn_values(b):
    return np.asarray(b, np.uint8).view(ml_dtypes.float8_e4m3fn).astype(np.float64)


def setup_inputs():
    d = draw0()
    x0 = np.asarray(d['dup_pool']).astype(np.float64)
    s = (np.max(np.abs(x0), axis=(0, 2), keepdims=True) / 448.0).astype(np.float32)
    out = {}
    for k, v in d.items():
        if k == 'dup_pool':
            out['dup_pool_bytes'] = e4m3fn_bytes(x0 / s.astype(np.float64))
            out['dup_pool_scale'] = s
        else:
            out[k] = v
    return out


def reference(ff_hid, tgt, w2, b2, g3, be3, dup_pool_bytes, dup_pool_scale, dup_bias):
    return core(ff_hid, tgt, w2, b2, g3, be3, e4m3fn_values(dup_pool_bytes) * dup_pool_scale.astype(np.float64), dup_bias)

@@ -1,0 +1,331 @@
+from contextlib import ExitStack
+
+import concourse.mybir as mybir
+from concourse.masks import make_identity
+
+B, K, G, D, FF = 16, 64, 128, 1024, 2048
+EPS = 1e-5
+FLOPS = 2 * B * K * FF * D + 2 * B * K * D * G
+
+F32 = mybir.dt.float32
+BF16 = mybir.dt.bfloat16
+I32 = mybir.dt.int32
+U8 = mybir.dt.uint8
+FP8 = mybir.dt.float8_e4m3fn
+FP8X4 = mybir.dt.float8_e4m3fn_x4
+ALU = mybir.AluOpType
+ACT = mybir.ActivationFunctionType
+
+P = 128
+TILES = 8
+HEADS = 8
+ZROW = P + B
+EDGE_V = 640
+W2_V = 512
+BUSY_V = 320
+FREE_V = 160
+
+
+def tile_mldecoder_pb_kernel(tc, ff_hid, tgt, w2, b2, g3, be3, dup_pool_bytes, dup_pool_scale, dup_bias, out):
+    nc = tc.nc
+    ff_rows = ff_hid.rearrange("b k f -> (b k) f").rearrange("(p i) f -> i p f", i=TILES)
+    tgt_rows = tgt.rearrange("b k d -> (b k) d").rearrange("(p i) d -> i p d", i=TILES)
+    w2_rows = w2.rearrange("(s p t) n -> s p t n", p=P, t=4)
+    dup_rows = dup_pool_bytes.rearrange("(j i) (s p t) g -> i s t p j g", i=TILES, s=2, t=4)
+
+    with ExitStack() as ctx:
+        keep = ctx.enter_context(tc.tile_pool(name="keep", bufs=1))
+        work = ctx.enter_context(tc.tile_pool(name="work", bufs=1))
+        psum = ctx.enter_context(tc.psum_pool(name="psum", bufs=1))
+
+        dscale = keep.tile([P, 2, 4], F32, name="dscale")
+        gain_bf = keep.tile([P, 2, 4], BF16, name="gain_bf")
+        shift_bf = keep.tile([P, 2, 4], BF16, name="shift_bf")
+        gain = keep.tile([P, 8], F32, name="gain")
+        shift = keep.tile([P, 8], F32, name="shift")
+        b2_rows = keep.tile([P, P], BF16, name="b2_rows")
+        b2_col = keep.tile([P, 8], F32, name="b2_col")
+        ident_f = keep.tile([P, P], F32, name="ident_f")
+        ident_b = keep.tile([P, P], BF16, name="ident_b")
+        obias = keep.tile([P, TILES, G], BF16, name="obias")
+        osb = keep.tile([P, TILES, G], F32, name="osb")
+        zpad = [keep.tile([P, 2, HEADS * ZROW], I32, name="zpad%d" % z, align_bytes=64) for z in range(2)]
+        w2_codes = [keep.tile([P, D], I32, name="w2_codes%d" % s, align_bytes=64) for s in range(4)]
+        w2_scales = [keep.tile([P, D], U8, name="w2_scales%d" % s, align_bytes=64) for s in range(4)]
+
+        st = {}
+
+        def load_dup(n):
+            for t in range(4):
+                raw = work.tile([P, HEADS, G], U8, name="dup_raw", bufs=16)
+                nc.sync.dma_start(out=raw[:], in_=dup_rows[n // 2, n % 2, t])
+                st["raw", n, t] = raw
+
+        def load_w2(s):
+            planes = work.tile([P, 4, D], BF16, name="planes", bufs=5, align_bytes=64)
+            nc.sync.dma_start(out=planes[:], in_=w2_rows[s])
+            st["w2", s] = planes
+
+        def load_ff(i):
+            ffr = work.tile([P, FF], BF16, name="ff_raw", bufs=3)
+            nc.sync.dma_start(out=ffr[:], in_=ff_rows[i])
+            st["ff", i] = ffr
+
+        def load_tgt(i):
+            tg = work.tile([P, D], BF16, name="tgt_raw", bufs=4)
+            nc.sync.dma_start(out=tg[:], in_=tgt_rows[i])
+            st["tgt", i] = tg
+
+        def widen(n, on_scalar=0):
+            planes = work.tile([P, 4, HEADS * G], BF16, name="planes", bufs=5, align_bytes=64)
+            for t in range(4):
+                col = dscale[:, n % 2, t : t + 1]
+                codes = st["raw", n, t][:].rearrange("p j g -> p (j g)").bitcast(FP8)
+                if t >= 4 - on_scalar:
+                    nc.scalar.activation(out=planes[:, t, :], in_=codes, func=ACT.Copy, scale=col)
+                else:
+                    nc.vector.tensor_scalar(out=planes[:, t, :], in0=codes, scalar1=col, scalar2=None, op0=ALU.mult)
+            st["planes", n] = planes
+
+        def interleave(key, planes, v_cols):
+            grouped = work.tile([P, 1024, 4], BF16, name="grouped", bufs=3, align_bytes=64)
+            src = planes[:].rearrange("p t (c i) -> p c t i", i=4)
+            dst = grouped[:].rearrange("p (c i) t -> p c t i", i=4)
+            cut = v_cols // 4
+            nc.scalar.copy(out=dst[:, cut:], in_=src[:, cut:])
+            nc.vector.tensor_copy(out=dst[:, :cut], in_=src[:, :cut])
+            st[key] = grouped
+
+        def quant(key, codes, scales):
+            nc.vector.quantize_mx(out=codes.bitcast(FP8X4), scales=scales, in_=st[key][:].rearrange("p c t -> p (c t)"))
+
+        def quant_dup(n):
+            codes = work.tile([P, HEADS * G], I32, name="dup_codes", bufs=5, align_bytes=64)
+            scales = work.tile([P, HEADS * G], U8, name="dup_scales", bufs=5, align_bytes=64)
+            flat = st["dup", n][:].rearrange("p c t -> p (c t)")
+            parts = 2 if n == 15 else 1
+            w = HEADS * G // parts
+            for h in range(parts):
+                nc.vector.quantize_mx(out=codes[:, h * w : (h + 1) * w].bitcast(FP8X4), scales=scales[:, h * w : (h + 1) * w],
+                                      in_=flat[:, 4 * h * w : 4 * (h + 1) * w])
+            st["dq", n] = (codes, scales)
+
+        def ff_turn(pair):
+            grouped = work.tile([P, 1024, 4], BF16, name="grouped", bufs=3, align_bytes=64)
+            words = grouped[:].rearrange("p c t -> p (c t)").bitcast(F32).rearrange("p (s r u) -> p s r u", s=4, u=2)
+            for a in range(2):
+                src = st["ff", 2 * pair + a][:].bitcast(F32)
+                for h in range(2):
+                    bank = psum.tile([P, 2, 2, P], F32, name="turn_bank", bufs=3)
+                    for s in range(2):
+                        for u in range(2):
+                            w0 = 256 * (2 * h + s)
+                            nc.tensor.transpose(bank[:, s, u, :], src[:, w0 + u : w0 + 256 : 2], ident_f[:])
+                    nc.scalar.copy(out=words[:, 2 * h : 2 * h + 2, a * P : (a + 1) * P, :], in_=bank[:].rearrange("p s u r -> p s r u"))
+            st["ffg", pair] = grouped
+
+        def ff_quant(pair):
+            codes = work.tile([P, 1024], I32, name="ff_codes", bufs=2, align_bytes=64)
+            scales = work.tile([P, 1024], U8, name="ff_scales", bufs=2, align_bytes=64)
+            quant(("ffg", pair), codes[:], scales[:])
+            st["ffq", pair] = (codes, scales)
+
+        def first_product(pair):
+            codes, scales = st["ffq", pair]
+            fft = work.tile([P, 8, 256], F32, name="fft", bufs=1)
+            for h in range(4):
+                bank = psum.tile([P, 2, 256], F32, name="mx1_bank", bufs=2)
+                for q in range(2):
+                    c = 2 * h + q
+                    for s in range(4):
+                        nc.tensor.matmul_mx(
+                            out=bank[:, q, :],
+                            lhsT=w2_codes[s][:, c * P : (c + 1) * P].bitcast(FP8X4),
+                            lhsT_scale=w2_scales[s][:, c * P : (c + 1) * P],
+                            rhs=codes[:, s * 256 : (s + 1) * 256].bitcast(FP8X4),
+                            rhs_scale=scales[:, s * 256 : (s + 1) * 256],
+                            start=(s == 0), stop=(s == 3))
+                for q in range(2):
+                    c = 2 * h + q
+                    nc.scalar.activation(out=fft[:, c, :], in_=bank[:, q, :], func=ACT.Identity, bias=b2_col[:, c : c + 1])
+            st["fft", pair] = fft
+
+        def residual(i):
+            fft = st["fft", i // 2]
+            a = i % 2
+            stats = work.tile([P, 2, 6], F32, name="stats", bufs=2)
+            banks = []
+            for h in range(2):
+                bank = psum.tile([P, 512], F32, name="u_bank", bufs=2)
+                nc.tensor.matmul(bank[:], lhsT=ident_b[:], rhs=st["tgt", i][:, h * 512 : (h + 1) * 512], start=True, stop=False)
+                for q in range(4):
+                    nc.tensor.matmul(bank[:, q * P : (q + 1) * P], lhsT=fft[:, 4 * h + q, a * P : (a + 1) * P], rhs=ident_f[:],
+                                     is_transpose=True, start=False, stop=(q == 3))
+                nc.vector.bn_stats(out=stats[:, h, :], in_=bank[:])
+                banks.append(bank)
+            mean_var = work.tile([P, 2], F32, name="mean_var", bufs=2)
+            nc.vector.bn_aggr(out=mean_var[:], in_=stats[:].rearrange("p h x -> p (h x)"))
+            std = work.tile([P, 1], F32, name="std", bufs=2)
+            nc.scalar.activation(out=std[:], in_=mean_var[:, 1:2], func=ACT.Sqrt, bias=EPS)
+            st["u", i] = (banks, mean_var, std)
+
+        def normalise(i):
+            banks, mean_var, std = st["u", i]
+            rstd = work.tile([P, 1], F32, name="rstd", bufs=2)
+            nc.vector.reciprocal(out=rstd[:], in_=std[:])
+            nbias = work.tile([P, 1], F32, name="nbias", bufs=2)
+            nc.vector.tensor_scalar(out=nbias[:], in0=mean_var[:, 0:1], scalar1=rstd[:], scalar2=-1.0, op0=ALU.mult, op1=ALU.mult)
+            normed = work.tile([P, 2, 4, P], F32, name="normed", bufs=3)
+            for h in range(2):
+                nc.scalar.activation(out=normed[:, h], in_=banks[h][:].rearrange("r (p t) -> r t p", t=4), func=ACT.Identity,
+                                     scale=rstd[:], bias=nbias[:])
+            st["n", i] = normed
+
+        def h_turn(pair):
+            hplanes = work.tile([P, 2, 4, 256], BF16, name="hplanes", bufs=1, align_bytes=64)
+            for s in range(2):
+                for th in range(2):
+                    bank = psum.tile([P, 2, 2, P], F32, name="turn_bank", bufs=3)
+                    for tt in range(2):
+                        for a in range(2):
+                            nc.tensor.transpose(bank[:, tt, a, :], st["n", 2 * pair + a][:, s, 2 * th + tt, :], ident_f[:])
+                    for tt in range(2):
+                        t = 2 * th + tt
+                        nc.scalar.activation(
+                            out=hplanes[:, s, t, :].rearrange("p (a j b) -> p a j b", a=2, j=HEADS),
+                            in_=bank[:, tt].rearrange("p a (b j) -> p a j b", j=HEADS),
+                            func=ACT.Identity, scale=gain[:, 4 * s + t : 4 * s + t + 1], bias=shift[:, 4 * s + t : 4 * s + t + 1])
+            st["hp", pair] = hplanes
+
+        def h_group(pair):
+            hgrouped = work.tile([P, 512, 4], BF16, name="hgrouped", bufs=1, align_bytes=64)
+            nc.vector.tensor_copy(
+                out=hgrouped[:].rearrange("p (s c i) t -> p s c t i", s=2, i=4),
+                in_=st["hp", pair][:].rearrange("p s t (c i) -> p s c t i", i=4))
+            st["hg", pair] = hgrouped
+
+        def h_quant(pair):
+            codes = work.tile([P, 512], I32, name="h_codes", bufs=3, align_bytes=64)
+            scales = work.tile([P, 512], U8, name="h_scales", bufs=3, align_bytes=64)
+            quant(("hg", pair), codes[:], scales[:])
+            st["hq", pair] = (codes, scales)
+
+        def spread(i):
+            codes = st["hq", i // 2][0]
+            nc.vector.tensor_copy(
+                out=zpad[i % 2][:].rearrange("p s (j x) -> p s j x", x=ZROW)[:, :, :, 0:B],
+                in_=codes[:].rearrange("p (s a j b) -> p s a j b", s=2, a=2, b=B)[:, :, i % 2])
+
+        def second_product(n):
+            i, s = n // 2, n % 2
+            if s == 0:
+                st["o", i] = psum.tile([P, G], F32, name="out_bank", bufs=1)
+            hscales = st["hq", i // 2][1]
+            codes, scales = st["dq", n]
+            c0 = s * 256 + (i % 2) * P
+            for j in range(HEADS):
+                nc.tensor.matmul_mx(
+                    out=st["o", i][:],
+                    lhsT=zpad[i % 2][:, s, j * P : (j + 1) * P].bitcast(FP8X4),
+                    lhsT_scale=hscales[:, c0 : c0 + P],
+                    rhs=codes[:, j * G : (j + 1) * G].bitcast(FP8X4),
+                    rhs_scale=scales[:, j * G : (j + 1) * G],
+                    start=(s == 0 and j == 0), stop=(s == 1 and j == HEADS - 1))
+
+        def finish(i):
+            nc.vector.tensor_tensor(out=osb[:, i, :], in0=st["o", i][:], in1=obias[:, i, :], op=ALU.add)
+
+        def store(i0, i1):
+            for j in range(HEADS):
+                nc.sync.dma_start(
+                    out=out[:, j * TILES * G + i0 * G : j * TILES * G + i1 * G],
+                    in_=osb[j * B : (j + 1) * B, i0:i1, :].rearrange("p i g -> p (i g)"))
+
+        nc.sync.dma_start(out=dscale[:], in_=dup_pool_scale.rearrange("o d z -> (o d z)").rearrange("(s p t) -> p s t", s=2, t=4))
+        load_dup(0)
+        warm = keep.tile([P, 1], F32, name="warm")
+        nc.vector.memset(warm[:], 1.0)
+        nc.scalar.activation(out=warm[:], in_=warm[:], func=ACT.Sqrt)
+        nc.gpsimd.memset(b2_rows[:], 0.0)
+        make_identity(nc, ident_f[:])
+        make_identity(nc, ident_b[:])
+        for z in range(2):
+            nc.vector.memset(zpad[z][:], 0)
+        load_w2(0)
+        load_w2(1)
+        load_ff(0)
+        load_ff(1)
+        nc.sync.dma_start(out=b2_rows[0:8, :], in_=b2.rearrange("(c p) -> c p", p=P))
+        load_dup(1)
+        load_w2(2)
+        load_w2(3)
+        nc.sync.dma_start(out=gain_bf[:], in_=g3.rearrange("(s p t) -> p s t", s=2, t=4))
+        nc.sync.dma_start(out=shift_bf[:], in_=be3.rearrange("(s p t) -> p s t", s=2, t=4))
+        load_tgt(0)
+        load_tgt(1)
+        load_dup(2)
+        load_dup(3)
+        widen(0, 1)
+        interleave(("dup", 0), st["planes", 0], EDGE_V)
+        b2_bank = psum.tile([P, P], BF16, name="out_bank", bufs=1)
+        nc.tensor.transpose(b2_bank[:], b2_rows[:], ident_b[:])
+        nc.scalar.copy(out=b2_col[:], in_=b2_bank[:, 0:8])
+        for s in range(4):
+            interleave(("w2g", s), st["w2", s], W2_V)
+            if s == 0:
+                quant_dup(0)
+            quant(("w2g", s), w2_codes[s][:], w2_scales[s][:])
+            if s == 1:
+                ff_turn(0)
+                ff_quant(0)
+        nc.scalar.copy(out=gain[:], in_=gain_bf[:].rearrange("p s t -> p (s t)"))
+        nc.scalar.copy(out=shift[:], in_=shift_bf[:].rearrange("p s t -> p (s t)"))
+        for j in range(HEADS):
+            nc.sync.dma_start(out=obias[j * B : (j + 1) * B].rearrange("p i g -> p (i g)"),
+                              in_=dup_bias[j * TILES * G : (j + 1) * TILES * G].partition_broadcast(B))
+
+        done = 0
+        for n in range(17):
+            pair, part = n // 3, n % 3
+            busy = pair < 4
+            if busy and part == 0:
+                first_product(pair)
+                if pair < 3:
+                    load_ff(2 * pair + 2)
+                    load_ff(2 * pair + 3)
+            if n >= 2:
+                quant_dup(n - 1)
+            if n + 1 < 16:
+                widen(n + 1)
+            if n + 4 < 16:
+                load_dup(n + 4)
+            if busy and part == 0:
+                residual(2 * pair)
+            if 0 < n < 16:
+                interleave(("dup", n), st["planes", n], EDGE_V if n == 15 else BUSY_V if busy else FREE_V)
+            if busy and part == 0:
+                normalise(2 * pair)
+            if busy and part == 1:
+                residual(2 * pair + 1)
+                if pair < 3:
+                    load_tgt(2 * pair + 2)
+                    load_tgt(2 * pair + 3)
+                    ff_turn(pair + 1)
+                normalise(2 * pair + 1)
+            if busy and part == 2:
+                h_turn(pair)
+                if pair < 3:
+                    ff_quant(pair + 1)
+                h_group(pair)
+                h_quant(pair)
+            ready = 4 * ((n + 1) // 3)
+            while done < min(n, ready):
+                if done % 2 == 0:
+                    spread(done // 2)
+                second_product(done)
+                if done % 2 == 1:
+                    finish(done // 2)
+                    if done == 13:
+                        store(0, 7)
+                done += 1
+        store(7, 8)

@@ -22,8 +22,7 @@ HEADS = 8
 ZROW = P + B
 EDGE_V = 640
 W2_V = 512
-BUSY_V = 320
-FREE_V = 160
+SHARES = (384, 224, 352, 160)
 
 
 def tile_mldecoder_pb_kernel(tc, ff_hid, tgt, w2, b2, g3, be3, dup_pool_bytes, dup_pool_scale, dup_bias, out):
@@ -37,6 +36,7 @@ def tile_mldecoder_pb_kernel(tc, ff_hid, tgt, w2, b2, g3, be3, dup_pool_bytes, d
         keep = ctx.enter_context(tc.tile_pool(name="keep", bufs=1))
         work = ctx.enter_context(tc.tile_pool(name="work", bufs=1))
         psum = ctx.enter_context(tc.psum_pool(name="psum", bufs=1))
+        ctx.enter_context(tc.manual_schedule())
 
         dscale = keep.tile([P, 2, 4], F32, name="dscale")
         gain_bf = keep.tile([P, 2, 4], BF16, name="gain_bf")
@@ -76,25 +76,19 @@ def tile_mldecoder_pb_kernel(tc, ff_hid, tgt, w2, b2, g3, be3, dup_pool_bytes, d
             nc.sync.dma_start(out=tg[:], in_=tgt_rows[i])
             st["tgt", i] = tg
 
-        def widen(n, on_scalar=0):
-            planes = work.tile([P, 4, HEADS * G], BF16, name="planes", bufs=5, align_bytes=64)
-            for t in range(4):
-                col = dscale[:, n % 2, t : t + 1]
-                codes = st["raw", n, t][:].rearrange("p j g -> p (j g)").bitcast(FP8)
-                if t >= 4 - on_scalar:
-                    nc.scalar.activation(out=planes[:, t, :], in_=codes, func=ACT.Copy, scale=col)
-                else:
-                    nc.vector.tensor_scalar(out=planes[:, t, :], in0=codes, scalar1=col, scalar2=None, op0=ALU.mult)
-            st["planes", n] = planes
+        def widen(n, t):
+            if t == 0:
+                st["planes", n] = work.tile([P, 4, HEADS * G], BF16, name="planes", bufs=5, align_bytes=64)
+            codes = st["raw", n, t][:].rearrange("p j g -> p (j g)").bitcast(FP8)
+            nc.vector.tensor_scalar(out=st["planes", n][:, t, :], in0=codes, scalar1=dscale[:, n % 2, t : t + 1], scalar2=None, op0=ALU.mult)
 
-        def interleave(key, planes, v_cols):
-            grouped = work.tile([P, 1024, 4], BF16, name="grouped", bufs=3, align_bytes=64)
+        def new_grouped(key):
+            st[key] = work.tile([P, 1024, 4], BF16, name="grouped", bufs=3, align_bytes=64)
+
+        def interleave(copy, key, planes, c0, c1):
             src = planes[:].rearrange("p t (c i) -> p c t i", i=4)
-            dst = grouped[:].rearrange("p (c i) t -> p c t i", i=4)
-            cut = v_cols // 4
-            nc.scalar.copy(out=dst[:, cut:], in_=src[:, cut:])
-            nc.vector.tensor_copy(out=dst[:, :cut], in_=src[:, :cut])
-            st[key] = grouped
+            dst = st[key][:].rearrange("p (c i) t -> p c t i", i=4)
+            copy(out=dst[:, c0 // 4 : c1 // 4], in_=src[:, c0 // 4 : c1 // 4])
 
         def quant(key, codes, scales):
             nc.vector.quantize_mx(out=codes.bitcast(FP8X4), scales=scales, in_=st[key][:].rearrange("p c t -> p (c t)"))
@@ -103,26 +97,27 @@ def tile_mldecoder_pb_kernel(tc, ff_hid, tgt, w2, b2, g3, be3, dup_pool_bytes, d
             codes = work.tile([P, HEADS * G], I32, name="dup_codes", bufs=5, align_bytes=64)
             scales = work.tile([P, HEADS * G], U8, name="dup_scales", bufs=5, align_bytes=64)
             flat = st["dup", n][:].rearrange("p c t -> p (c t)")
-            parts = 2 if n == 15 else 1
+            parts = 1
             w = HEADS * G // parts
             for h in range(parts):
                 nc.vector.quantize_mx(out=codes[:, h * w : (h + 1) * w].bitcast(FP8X4), scales=scales[:, h * w : (h + 1) * w],
                                       in_=flat[:, 4 * h * w : 4 * (h + 1) * w])
             st["dq", n] = (codes, scales)
 
-        def ff_turn(pair):
-            grouped = work.tile([P, 1024, 4], BF16, name="grouped", bufs=3, align_bytes=64)
-            words = grouped[:].rearrange("p c t -> p (c t)").bitcast(F32).rearrange("p (s r u) -> p s r u", s=4, u=2)
-            for a in range(2):
-                src = st["ff", 2 * pair + a][:].bitcast(F32)
-                for h in range(2):
-                    bank = psum.tile([P, 2, 2, P], F32, name="turn_bank", bufs=3)
-                    for s in range(2):
-                        for u in range(2):
-                            w0 = 256 * (2 * h + s)
-                            nc.tensor.transpose(bank[:, s, u, :], src[:, w0 + u : w0 + 256 : 2], ident_f[:])
-                    nc.scalar.copy(out=words[:, 2 * h : 2 * h + 2, a * P : (a + 1) * P, :], in_=bank[:].rearrange("p s u r -> p s r u"))
-            st["ffg", pair] = grouped
+        def ff_turn(pair, a):
+            src = st["ff", 2 * pair + a][:].bitcast(F32)
+            for h in range(2):
+                bank = psum.tile([P, 2, 2, P], F32, name="bank", bufs=6)
+                for s in range(2):
+                    for u in range(2):
+                        w0 = 256 * (2 * h + s)
+                        nc.tensor.transpose(bank[:, s, u, :], src[:, w0 + u : w0 + 256 : 2], ident_f[:])
+                st["ffb", pair, a, h] = bank
+
+        def ff_copy(pair, a):
+            words = st["ffg", pair][:].rearrange("p c t -> p (c t)").bitcast(F32).rearrange("p (s r u) -> p s r u", s=4, u=2)
+            for h in range(2):
+                nc.scalar.copy(out=words[:, 2 * h : 2 * h + 2, a * P : (a + 1) * P, :], in_=st["ffb", pair, a, h][:].rearrange("p s u r -> p s r u"))
 
         def ff_quant(pair):
             codes = work.tile([P, 1024], I32, name="ff_codes", bufs=2, align_bytes=64)
@@ -130,72 +125,84 @@ def tile_mldecoder_pb_kernel(tc, ff_hid, tgt, w2, b2, g3, be3, dup_pool_bytes, d
             quant(("ffg", pair), codes[:], scales[:])
             st["ffq", pair] = (codes, scales)
 
-        def first_product(pair):
+        def first_product(pair, h):
             codes, scales = st["ffq", pair]
-            fft = work.tile([P, 8, 256], F32, name="fft", bufs=1)
-            for h in range(4):
-                bank = psum.tile([P, 2, 256], F32, name="mx1_bank", bufs=2)
-                for q in range(2):
-                    c = 2 * h + q
-                    for s in range(4):
-                        nc.tensor.matmul_mx(
-                            out=bank[:, q, :],
-                            lhsT=w2_codes[s][:, c * P : (c + 1) * P].bitcast(FP8X4),
-                            lhsT_scale=w2_scales[s][:, c * P : (c + 1) * P],
-                            rhs=codes[:, s * 256 : (s + 1) * 256].bitcast(FP8X4),
-                            rhs_scale=scales[:, s * 256 : (s + 1) * 256],
-                            start=(s == 0), stop=(s == 3))
-                for q in range(2):
-                    c = 2 * h + q
-                    nc.scalar.activation(out=fft[:, c, :], in_=bank[:, q, :], func=ACT.Identity, bias=b2_col[:, c : c + 1])
-            st["fft", pair] = fft
+            bank = psum.tile([P, 2, 256], F32, name="bank", bufs=6)
+            for q in range(2):
+                c = 2 * h + q
+                for s in range(4):
+                    nc.tensor.matmul_mx(
+                        out=bank[:, q, :],
+                        lhsT=w2_codes[s][:, c * P : (c + 1) * P].bitcast(FP8X4),
+                        lhsT_scale=w2_scales[s][:, c * P : (c + 1) * P],
+                        rhs=codes[:, s * 256 : (s + 1) * 256].bitcast(FP8X4),
+                        rhs_scale=scales[:, s * 256 : (s + 1) * 256],
+                        start=(s == 0), stop=(s == 3))
+            st["mx1", pair, h] = bank
 
-        def residual(i):
-            fft = st["fft", i // 2]
-            a = i % 2
-            stats = work.tile([P, 2, 6], F32, name="stats", bufs=2)
-            banks = []
+        def add_b2(pair, h):
+            if h == 0:
+                st["fft", pair] = work.tile([P, 8, 256], F32, name="fft", bufs=1)
+            for q in range(2):
+                c = 2 * h + q
+                nc.scalar.activation(out=st["fft", pair][:, c, :], in_=st["mx1", pair, h][:, q, :], func=ACT.Identity, bias=b2_col[:, c : c + 1])
+
+        def residual(pair, a, h):
+            bank = psum.tile([P, 512], F32, name="bank", bufs=6)
+            nc.tensor.matmul(bank[:], lhsT=ident_b[:], rhs=st["tgt", 2 * pair + a][:, h * 512 : (h + 1) * 512], start=True, stop=False)
+            for q in range(4):
+                nc.tensor.matmul(bank[:, q * P : (q + 1) * P], lhsT=st["fft", pair][:, 4 * h + q, a * P : (a + 1) * P], rhs=ident_f[:],
+                                 is_transpose=True, start=False, stop=(q == 3))
+            st["u", pair, a, h] = bank
+
+        def moments(pair):
+            stats = work.tile([P, 2, 2, 6], F32, name="stats", bufs=2)
+            mean_var = work.tile([P, 2, 2], F32, name="mean_var", bufs=2)
+            for a in range(2):
+                for h in range(2):
+                    nc.vector.bn_stats(out=stats[:, a, h, :], in_=st["u", pair, a, h][:])
+            for a in range(2):
+                nc.vector.bn_aggr(out=mean_var[:, a, :], in_=stats[:, a].rearrange("p h x -> p (h x)"))
+            st["mv", pair] = mean_var
+
+        def deviation(pair):
+            std = work.tile([P, 2], F32, name="std", bufs=2)
+            nc.scalar.activation(out=std[:], in_=st["mv", pair][:, :, 1], func=ACT.Sqrt, bias=EPS)
+            st["std", pair] = std
+
+        def inverse(pair):
+            rstd = work.tile([P, 2], F32, name="rstd", bufs=2)
+            nc.vector.reciprocal(out=rstd[:], in_=st["std", pair][:])
+            st["rstd", pair] = rstd
+
+        def offset(pair):
+            nbias = work.tile([P, 2], F32, name="nbias", bufs=2)
+            nc.vector.scalar_tensor_tensor(out=nbias[:], in0=st["mv", pair][:, :, 0], scalar=-1.0, in1=st["rstd", pair][:], op0=ALU.mult, op1=ALU.mult)
+            st["nbias", pair] = nbias
+
+        def normalise(pair, a):
+            normed = work.tile([P, 2, 4, P], F32, name="normed", bufs=2)
             for h in range(2):
-                bank = psum.tile([P, 512], F32, name="u_bank", bufs=2)
-                nc.tensor.matmul(bank[:], lhsT=ident_b[:], rhs=st["tgt", i][:, h * 512 : (h + 1) * 512], start=True, stop=False)
-                for q in range(4):
-                    nc.tensor.matmul(bank[:, q * P : (q + 1) * P], lhsT=fft[:, 4 * h + q, a * P : (a + 1) * P], rhs=ident_f[:],
-                                     is_transpose=True, start=False, stop=(q == 3))
-                nc.vector.bn_stats(out=stats[:, h, :], in_=bank[:])
-                banks.append(bank)
-            mean_var = work.tile([P, 2], F32, name="mean_var", bufs=2)
-            nc.vector.bn_aggr(out=mean_var[:], in_=stats[:].rearrange("p h x -> p (h x)"))
-            std = work.tile([P, 1], F32, name="std", bufs=2)
-            nc.scalar.activation(out=std[:], in_=mean_var[:, 1:2], func=ACT.Sqrt, bias=EPS)
-            st["u", i] = (banks, mean_var, std)
+                nc.scalar.activation(out=normed[:, h], in_=st["u", pair, a, h][:].rearrange("r (p t) -> r t p", t=4), func=ACT.Identity,
+                                     scale=st["rstd", pair][:, a : a + 1], bias=st["nbias", pair][:, a : a + 1])
+            st["n", pair, a] = normed
 
-        def normalise(i):
-            banks, mean_var, std = st["u", i]
-            rstd = work.tile([P, 1], F32, name="rstd", bufs=2)
-            nc.vector.reciprocal(out=rstd[:], in_=std[:])
-            nbias = work.tile([P, 1], F32, name="nbias", bufs=2)
-            nc.vector.tensor_scalar(out=nbias[:], in0=mean_var[:, 0:1], scalar1=rstd[:], scalar2=-1.0, op0=ALU.mult, op1=ALU.mult)
-            normed = work.tile([P, 2, 4, P], F32, name="normed", bufs=3)
-            for h in range(2):
-                nc.scalar.activation(out=normed[:, h], in_=banks[h][:].rearrange("r (p t) -> r t p", t=4), func=ACT.Identity,
-                                     scale=rstd[:], bias=nbias[:])
-            st["n", i] = normed
+        def h_turn(pair, s):
+            for th in range(2):
+                bank = psum.tile([P, 2, 2, P], F32, name="bank", bufs=6)
+                for tt in range(2):
+                    for a in range(2):
+                        nc.tensor.transpose(bank[:, tt, a, :], st["n", pair, a][:, s, 2 * th + tt, :], ident_f[:])
+                st["hb", pair, s, th] = bank
 
-        def h_turn(pair):
-            hplanes = work.tile([P, 2, 4, 256], BF16, name="hplanes", bufs=1, align_bytes=64)
-            for s in range(2):
-                for th in range(2):
-                    bank = psum.tile([P, 2, 2, P], F32, name="turn_bank", bufs=3)
-                    for tt in range(2):
-                        for a in range(2):
-                            nc.tensor.transpose(bank[:, tt, a, :], st["n", 2 * pair + a][:, s, 2 * th + tt, :], ident_f[:])
-                    for tt in range(2):
-                        t = 2 * th + tt
-                        nc.scalar.activation(
-                            out=hplanes[:, s, t, :].rearrange("p (a j b) -> p a j b", a=2, j=HEADS),
-                            in_=bank[:, tt].rearrange("p a (b j) -> p a j b", j=HEADS),
-                            func=ACT.Identity, scale=gain[:, 4 * s + t : 4 * s + t + 1], bias=shift[:, 4 * s + t : 4 * s + t + 1])
-            st["hp", pair] = hplanes
+        def affine(pair, s):
+            if s == 0:
+                st["hp", pair] = work.tile([P, 2, 4, 256], BF16, name="hplanes", bufs=1, align_bytes=64)
+            for t in range(4):
+                nc.scalar.activation(
+                    out=st["hp", pair][:, s, t, :].rearrange("p (a j b) -> p a j b", a=2, j=HEADS),
+                    in_=st["hb", pair, s, t // 2][:, t % 2].rearrange("p a (b j) -> p a j b", j=HEADS),
+                    func=ACT.Identity, scale=gain[:, 4 * s + t : 4 * s + t + 1], bias=shift[:, 4 * s + t : 4 * s + t + 1])
 
         def h_group(pair):
             hgrouped = work.tile([P, 512, 4], BF16, name="hgrouped", bufs=1, align_bytes=64)
@@ -219,7 +226,7 @@ def tile_mldecoder_pb_kernel(tc, ff_hid, tgt, w2, b2, g3, be3, dup_pool_bytes, d
         def second_product(n):
             i, s = n // 2, n % 2
             if s == 0:
-                st["o", i] = psum.tile([P, G], F32, name="out_bank", bufs=1)
+                st["o", i] = psum.tile([P, G], F32, name="out_bank", bufs=2)
             hscales = st["hq", i // 2][1]
             codes, scales = st["dq", n]
             c0 = s * 256 + (i % 2) * P
@@ -242,7 +249,6 @@ def tile_mldecoder_pb_kernel(tc, ff_hid, tgt, w2, b2, g3, be3, dup_pool_bytes, d
                     in_=osb[j * B : (j + 1) * B, i0:i1, :].rearrange("p i g -> p (i g)"))
 
         nc.sync.dma_start(out=dscale[:], in_=dup_pool_scale.rearrange("o d z -> (o d z)").rearrange("(s p t) -> p s t", s=2, t=4))
-        load_dup(0)
         warm = keep.tile([P, 1], F32, name="warm")
         nc.vector.memset(warm[:], 1.0)
         nc.scalar.activation(out=warm[:], in_=warm[:], func=ACT.Sqrt)
@@ -256,76 +262,146 @@ def tile_mldecoder_pb_kernel(tc, ff_hid, tgt, w2, b2, g3, be3, dup_pool_bytes, d
         load_ff(0)
         load_ff(1)
         nc.sync.dma_start(out=b2_rows[0:8, :], in_=b2.rearrange("(c p) -> c p", p=P))
-        load_dup(1)
         load_w2(2)
         load_w2(3)
-        nc.sync.dma_start(out=gain_bf[:], in_=g3.rearrange("(s p t) -> p s t", s=2, t=4))
-        nc.sync.dma_start(out=shift_bf[:], in_=be3.rearrange("(s p t) -> p s t", s=2, t=4))
+        load_dup(0)
+        load_dup(1)
         load_tgt(0)
         load_tgt(1)
+        nc.sync.dma_start(out=gain_bf[:], in_=g3.rearrange("(s p t) -> p s t", s=2, t=4))
+        nc.sync.dma_start(out=shift_bf[:], in_=be3.rearrange("(s p t) -> p s t", s=2, t=4))
         load_dup(2)
         load_dup(3)
-        widen(0, 1)
-        interleave(("dup", 0), st["planes", 0], EDGE_V)
-        b2_bank = psum.tile([P, P], BF16, name="out_bank", bufs=1)
+        ff_turn(0, 0)
+        ff_turn(0, 1)
+        b2_bank = psum.tile([P, P], BF16, name="bank", bufs=6)
         nc.tensor.transpose(b2_bank[:], b2_rows[:], ident_b[:])
-        nc.scalar.copy(out=b2_col[:], in_=b2_bank[:, 0:8])
         for s in range(4):
-            interleave(("w2g", s), st["w2", s], W2_V)
-            if s == 0:
-                quant_dup(0)
-            quant(("w2g", s), w2_codes[s][:], w2_scales[s][:])
+            new_grouped(("w2g", s))
+            interleave(nc.vector.tensor_copy, ("w2g", s), st["w2", s], 0, W2_V)
+            interleave(nc.scalar.copy, ("w2g", s), st["w2", s], W2_V, D)
+            if s > 0:
+                quant(("w2g", s - 1), w2_codes[s - 1][:], w2_scales[s - 1][:])
             if s == 1:
-                ff_turn(0)
+                new_grouped(("ffg", 0))
+                ff_copy(0, 0)
+                ff_copy(0, 1)
+            if s == 2:
                 ff_quant(0)
-        nc.scalar.copy(out=gain[:], in_=gain_bf[:].rearrange("p s t -> p (s t)"))
-        nc.scalar.copy(out=shift[:], in_=shift_bf[:].rearrange("p s t -> p (s t)"))
-        for j in range(HEADS):
-            nc.sync.dma_start(out=obias[j * B : (j + 1) * B].rearrange("p i g -> p (i g)"),
-                              in_=dup_bias[j * TILES * G : (j + 1) * TILES * G].partition_broadcast(B))
+        widen(0, 0)
+        quant(("w2g", 3), w2_codes[3][:], w2_scales[3][:])
+        for t in range(1, 4):
+            widen(0, t)
+        nc.scalar.copy(out=b2_col[:], in_=b2_bank[:, 0:8])
 
-        done = 0
-        for n in range(17):
-            pair, part = n // 3, n % 3
-            busy = pair < 4
-            if busy and part == 0:
-                first_product(pair)
+        for n in range(16):
+            pair, part = divmod(n, 4)
+            share = SHARES[part] if n < 15 else EDGE_V
+            mid = (share + D) // 64 * 32
+            key = ("dup", n)
+            more = n < 15
+
+            def wide(t):
+                if more:
+                    widen(n + 1, t)
+
+            if part == 3 and more:
+                new_grouped(("ffg", pair + 1))
+            new_grouped(key)
+            if n + 4 < 16:
+                load_dup(n + 4)
+            if n == 0:
+                for j in range(HEADS):
+                    nc.sync.dma_start(out=obias[j * B : (j + 1) * B].rearrange("p i g -> p (i g)"),
+                                      in_=dup_bias[j * TILES * G : (j + 1) * TILES * G].partition_broadcast(B))
+            if part == 0:
                 if pair < 3:
                     load_ff(2 * pair + 2)
                     load_ff(2 * pair + 3)
-            if n >= 2:
-                quant_dup(n - 1)
-            if n + 1 < 16:
-                widen(n + 1)
-            if n + 4 < 16:
-                load_dup(n + 4)
-            if busy and part == 0:
-                residual(2 * pair)
-            if 0 < n < 16:
-                interleave(("dup", n), st["planes", n], EDGE_V if n == 15 else BUSY_V if busy else FREE_V)
-            if busy and part == 0:
-                normalise(2 * pair)
-            if busy and part == 1:
-                residual(2 * pair + 1)
+                if pair == 0:
+                    for h in range(4):
+                        first_product(pair, h)
+                interleave(nc.scalar.copy, key, st["planes", n], share, mid)
+                for h in range(4):
+                    add_b2(pair, h)
+                interleave(nc.scalar.copy, key, st["planes", n], mid, D)
+                for h in range(2):
+                    for a in range(2):
+                        residual(pair, a, h)
+                wide(0)
+                wide(1)
+                if n > 0:
+                    quant_dup(n - 1)
+                    second_product(n - 1)
+                wide(2)
+                wide(3)
+                interleave(nc.vector.tensor_copy, key, st["planes", n], 0, share)
+            if part == 1:
                 if pair < 3:
                     load_tgt(2 * pair + 2)
                     load_tgt(2 * pair + 3)
-                    ff_turn(pair + 1)
-                normalise(2 * pair + 1)
-            if busy and part == 2:
-                h_turn(pair)
+                moments(pair)
+                interleave(nc.scalar.copy, key, st["planes", n], share, mid)
+                deviation(pair)
+                wide(0)
+                inverse(pair)
+                wide(1)
+                offset(pair)
+                quant_dup(n - 1)
+                interleave(nc.scalar.copy, key, st["planes", n], mid, D)
+                if pair == 0:
+                    nc.scalar.copy(out=gain[:], in_=gain_bf[:].rearrange("p s t -> p (s t)"))
+                    nc.scalar.copy(out=shift[:], in_=shift_bf[:].rearrange("p s t -> p (s t)"))
+                normalise(pair, 0)
+                normalise(pair, 1)
+                wide(2)
+                wide(3)
+                if pair > 0:
+                    finish(2 * pair - 1)
+                if pair > 1:
+                    store(0 if pair == 2 else 4, 2 * pair)
+                interleave(nc.vector.tensor_copy, key, st["planes", n], 0, share)
+            if part == 2:
+                h_turn(pair, 0)
+                h_turn(pair, 1)
+                interleave(nc.scalar.copy, key, st["planes", n], share, mid)
+                affine(pair, 0)
+                affine(pair, 1)
                 if pair < 3:
-                    ff_quant(pair + 1)
+                    ff_turn(pair + 1, 0)
+                    ff_turn(pair + 1, 1)
+                interleave(nc.scalar.copy, key, st["planes", n], mid, D)
+                wide(0)
+                wide(1)
+                quant_dup(n - 1)
+                wide(2)
+                wide(3)
+                interleave(nc.vector.tensor_copy, key, st["planes", n], 0, share)
+            if part == 3:
+                if more:
+                    ff_copy(pair + 1, 0)
+                    ff_copy(pair + 1, 1)
+                interleave(nc.scalar.copy, key, st["planes", n], share, D)
                 h_group(pair)
+                wide(0)
                 h_quant(pair)
-            ready = 4 * ((n + 1) // 3)
-            while done < min(n, ready):
-                if done % 2 == 0:
-                    spread(done // 2)
-                second_product(done)
-                if done % 2 == 1:
-                    finish(done // 2)
-                    if done == 13:
-                        store(0, 7)
-                done += 1
-        store(7, 8)
+                wide(1)
+                spread(2 * pair)
+                spread(2 * pair + 1)
+                if more:
+                    ff_quant(pair + 1)
+                second_product(n - 3)
+                second_product(n - 2)
+                if more:
+                    for h in range(4):
+                        first_product(pair + 1, h)
+                quant_dup(n - 1)
+                second_product(n - 1)
+                wide(2)
+                wide(3)
+                interleave(nc.vector.tensor_copy, key, st["planes", n], 0, share)
+                finish(2 * pair)
+        quant_dup(15)
+        second_product(15)
+        finish(7)
+        store(6, 8)

@@ -20,16 +20,17 @@ P = 128
 TILES = 8
 HEADS = 8
 ZROW = P + B
-EDGE_V = 640
+HEAD_V = 384
+EDGE_V = 512
 W2_V = 512
-SHARES = (384, 224, 352, 160)
+SHARES = (256, 512, 320, 160)
 
 
 def tile_mldecoder_pb_kernel(tc, ff_hid, tgt, w2, b2, g3, be3, dup_pool_bytes, dup_pool_scale, dup_bias, out):
     nc = tc.nc
     ff_rows = ff_hid.rearrange("b k f -> (b k) f").rearrange("(p i) f -> i p f", i=TILES)
     tgt_rows = tgt.rearrange("b k d -> (b k) d").rearrange("(p i) d -> i p d", i=TILES)
-    w2_rows = w2.rearrange("(s p t) n -> s p t n", p=P, t=4)
+    w2_rows = w2.rearrange("(s p t) (hf n) -> hf s p t n", p=P, t=4, hf=2)
     dup_rows = dup_pool_bytes.rearrange("(j i) (s p t) g -> i s t p j g", i=TILES, s=2, t=4)
 
     with ExitStack() as ctx:
@@ -62,8 +63,9 @@ def tile_mldecoder_pb_kernel(tc, ff_hid, tgt, w2, b2, g3, be3, dup_pool_bytes, d
                 st["raw", n, t] = raw
 
         def load_w2(s):
-            planes = work.tile([P, 4, D], BF16, name="planes", bufs=5, align_bytes=64)
-            nc.sync.dma_start(out=planes[:], in_=w2_rows[s])
+            planes = work.tile([P, 4, D], BF16, name="planes", bufs=6, align_bytes=64)
+            for ss in range(2):
+                nc.sync.dma_start(out=planes[:, :, ss * 512 : (ss + 1) * 512], in_=w2_rows[s // 2, 2 * (s % 2) + ss])
             st["w2", s] = planes
 
         def load_ff(i):
@@ -78,9 +80,13 @@ def tile_mldecoder_pb_kernel(tc, ff_hid, tgt, w2, b2, g3, be3, dup_pool_bytes, d
 
         def widen(n, t):
             if t == 0:
-                st["planes", n] = work.tile([P, 4, HEADS * G], BF16, name="planes", bufs=5, align_bytes=64)
+                st["planes", n] = work.tile([P, 4, HEADS * G], BF16, name="planes", bufs=6, align_bytes=64)
             codes = st["raw", n, t][:].rearrange("p j g -> p (j g)").bitcast(FP8)
             nc.vector.tensor_scalar(out=st["planes", n][:, t, :], in0=codes, scalar1=dscale[:, n % 2, t : t + 1], scalar2=None, op0=ALU.mult)
+
+        def widen_on_scalar(n, t):
+            codes = st["raw", n, t][:].rearrange("p j g -> p (j g)").bitcast(FP8)
+            nc.scalar.activation(out=st["planes", n][:, t, :], in_=codes, func=ACT.Copy, scale=dscale[:, n % 2, t : t + 1])
 
         def new_grouped(key):
             st[key] = work.tile([P, 1024, 4], BF16, name="grouped", bufs=3, align_bytes=64)
@@ -94,10 +100,10 @@ def tile_mldecoder_pb_kernel(tc, ff_hid, tgt, w2, b2, g3, be3, dup_pool_bytes, d
             nc.vector.quantize_mx(out=codes.bitcast(FP8X4), scales=scales, in_=st[key][:].rearrange("p c t -> p (c t)"))
 
         def quant_dup(n):
-            codes = work.tile([P, HEADS * G], I32, name="dup_codes", bufs=5, align_bytes=64)
-            scales = work.tile([P, HEADS * G], U8, name="dup_scales", bufs=5, align_bytes=64)
+            codes = work.tile([P, HEADS * G], I32, name="dup_codes", bufs=6, align_bytes=64)
+            scales = work.tile([P, HEADS * G], U8, name="dup_scales", bufs=6, align_bytes=64)
             flat = st["dup", n][:].rearrange("p c t -> p (c t)")
-            parts = 1
+            parts = 2 if n == 15 else 1
             w = HEADS * G // parts
             for h in range(parts):
                 nc.vector.quantize_mx(out=codes[:, h * w : (h + 1) * w].bitcast(FP8X4), scales=scales[:, h * w : (h + 1) * w],
@@ -131,10 +137,11 @@ def tile_mldecoder_pb_kernel(tc, ff_hid, tgt, w2, b2, g3, be3, dup_pool_bytes, d
             for q in range(2):
                 c = 2 * h + q
                 for s in range(4):
+                    unit, c0 = 2 * (c // 4) + s // 2, (s % 2) * 512 + (c % 4) * P
                     nc.tensor.matmul_mx(
                         out=bank[:, q, :],
-                        lhsT=w2_codes[s][:, c * P : (c + 1) * P].bitcast(FP8X4),
-                        lhsT_scale=w2_scales[s][:, c * P : (c + 1) * P],
+                        lhsT=w2_codes[unit][:, c0 : c0 + P].bitcast(FP8X4),
+                        lhsT_scale=w2_scales[unit][:, c0 : c0 + P],
                         rhs=codes[:, s * 256 : (s + 1) * 256].bitcast(FP8X4),
                         rhs_scale=scales[:, s * 256 : (s + 1) * 256],
                         start=(s == 0), stop=(s == 3))
@@ -244,7 +251,8 @@ def tile_mldecoder_pb_kernel(tc, ff_hid, tgt, w2, b2, g3, be3, dup_pool_bytes, d
 
         def store(i0, i1):
             for j in range(HEADS):
-                nc.sync.dma_start(
+                queue = nc.scalar if i1 == 8 and j % 2 else nc.sync
+                queue.dma_start(
                     out=out[:, j * TILES * G + i0 * G : j * TILES * G + i1 * G],
                     in_=osb[j * B : (j + 1) * B, i0:i1, :].rearrange("p i g -> p (i g)"))
 
@@ -257,151 +265,201 @@ def tile_mldecoder_pb_kernel(tc, ff_hid, tgt, w2, b2, g3, be3, dup_pool_bytes, d
         make_identity(nc, ident_b[:])
         for z in range(2):
             nc.vector.memset(zpad[z][:], 0)
+        load_dup(0)
         load_w2(0)
+        load_dup(1)
         load_w2(1)
         load_ff(0)
         load_ff(1)
         nc.sync.dma_start(out=b2_rows[0:8, :], in_=b2.rearrange("(c p) -> c p", p=P))
         load_w2(2)
+        load_dup(2)
         load_w2(3)
-        load_dup(0)
-        load_dup(1)
         load_tgt(0)
         load_tgt(1)
+        load_dup(3)
         nc.sync.dma_start(out=gain_bf[:], in_=g3.rearrange("(s p t) -> p s t", s=2, t=4))
         nc.sync.dma_start(out=shift_bf[:], in_=be3.rearrange("(s p t) -> p s t", s=2, t=4))
-        load_dup(2)
-        load_dup(3)
         ff_turn(0, 0)
         ff_turn(0, 1)
+        load_ff(2)
+        load_ff(3)
         b2_bank = psum.tile([P, P], BF16, name="bank", bufs=6)
         nc.tensor.transpose(b2_bank[:], b2_rows[:], ident_b[:])
-        for s in range(4):
-            new_grouped(("w2g", s))
-            interleave(nc.vector.tensor_copy, ("w2g", s), st["w2", s], 0, W2_V)
-            interleave(nc.scalar.copy, ("w2g", s), st["w2", s], W2_V, D)
-            if s > 0:
-                quant(("w2g", s - 1), w2_codes[s - 1][:], w2_scales[s - 1][:])
-            if s == 1:
-                new_grouped(("ffg", 0))
-                ff_copy(0, 0)
-                ff_copy(0, 1)
-            if s == 2:
-                ff_quant(0)
-        widen(0, 0)
-        quant(("w2g", 3), w2_codes[3][:], w2_scales[3][:])
-        for t in range(1, 4):
-            widen(0, t)
-        nc.scalar.copy(out=b2_col[:], in_=b2_bank[:, 0:8])
 
-        for n in range(16):
-            pair, part = divmod(n, 4)
+        def both(key, planes, share):
+            new_grouped(key)
+            interleave(nc.vector.tensor_copy, key, planes, 0, share)
+            interleave(nc.scalar.copy, key, planes, share, D)
+
+        def quant_w2(s):
+            quant(("w2g", s), w2_codes[s][:], w2_scales[s][:])
+
+        for t in range(4):
+            if t % 2 == 1:
+                widen_on_scalar(0, t)
+            else:
+                widen(0, t)
+        both(("dup", 0), st["planes", 0], W2_V)
+        both(("w2g", 0), st["w2", 0], W2_V)
+        for t in range(4):
+            widen(1, t)
+        load_dup(4)
+        quant_dup(0)
+        both(("dup", 1), st["planes", 1], HEAD_V)
+        quant_w2(0)
+        both(("w2g", 1), st["w2", 1], W2_V)
+        quant_dup(1)
+        new_grouped(("ffg", 0))
+        ff_copy(0, 0)
+        ff_copy(0, 1)
+        nc.scalar.copy(out=b2_col[:], in_=b2_bank[:, 0:8])
+        quant_w2(1)
+        both(("w2g", 2), st["w2", 2], W2_V)
+        ff_quant(0)
+        first_product(0, 0)
+        first_product(0, 1)
+        for t in range(4):
+            widen(2, t)
+        quant_w2(2)
+        both(("w2g", 3), st["w2", 3], W2_V)
+        add_b2(0, 0)
+        add_b2(0, 1)
+        quant_w2(3)
+        first_product(0, 2)
+        first_product(0, 3)
+
+        multiplied = 0
+        finished = 0
+        for n in range(2, 17):
+            pair, part = divmod(n - 2, 3)
+            if pair > 3:
+                part = 3
             share = SHARES[part] if n < 15 else EDGE_V
             mid = (share + D) // 64 * 32
             key = ("dup", n)
-            more = n < 15
 
             def wide(t):
-                if more:
+                if n < 15:
                     widen(n + 1, t)
 
-            if part == 3 and more:
+            def mix(copy, c0, c1):
+                if n < 16:
+                    interleave(copy, key, st["planes", n], c0, c1)
+
+            closed = multiplied // 2
+            ready = [c for c in range(multiplied, n) if 3 * (c // 4) + 4 < n]
+            multiplied += len(ready)
+
+            def products():
+                for c in ready:
+                    if c % 2 == 0:
+                        spread(c // 2)
+                    second_product(c)
+
+            if part == 1 and pair < 3:
                 new_grouped(("ffg", pair + 1))
-            new_grouped(key)
-            if n + 4 < 16:
-                load_dup(n + 4)
-            if n == 0:
+            if n < 16:
+                new_grouped(key)
+            if n + 3 < 16:
+                load_dup(n + 3)
+            if n == 2:
                 for j in range(HEADS):
                     nc.sync.dma_start(out=obias[j * B : (j + 1) * B].rearrange("p i g -> p (i g)"),
                                       in_=dup_bias[j * TILES * G : (j + 1) * TILES * G].partition_broadcast(B))
             if part == 0:
-                if pair < 3:
-                    load_ff(2 * pair + 2)
-                    load_ff(2 * pair + 3)
-                if pair == 0:
-                    for h in range(4):
-                        first_product(pair, h)
-                interleave(nc.scalar.copy, key, st["planes", n], share, mid)
-                for h in range(4):
-                    add_b2(pair, h)
-                interleave(nc.scalar.copy, key, st["planes", n], mid, D)
+                if pair > 0:
+                    add_b2(pair, 0)
+                    add_b2(pair, 1)
+                mix(nc.scalar.copy, share, mid)
+                add_b2(pair, 2)
+                add_b2(pair, 3)
+                mix(nc.scalar.copy, mid, D)
                 for h in range(2):
                     for a in range(2):
                         residual(pair, a, h)
+                if pair < 3:
+                    ff_turn(pair + 1, 0)
                 wide(0)
+                if pair > 0:
+                    h_quant(pair - 1)
                 wide(1)
-                if n > 0:
+                if pair > 0:
                     quant_dup(n - 1)
-                    second_product(n - 1)
+                products()
                 wide(2)
                 wide(3)
-                interleave(nc.vector.tensor_copy, key, st["planes", n], 0, share)
             if part == 1:
                 if pair < 3:
                     load_tgt(2 * pair + 2)
                     load_tgt(2 * pair + 3)
+                    ff_copy(pair + 1, 0)
+                    ff_turn(pair + 1, 1)
                 moments(pair)
-                interleave(nc.scalar.copy, key, st["planes", n], share, mid)
+                mix(nc.scalar.copy, share, mid)
                 deviation(pair)
+                mix(nc.scalar.copy, mid, D)
                 wide(0)
                 inverse(pair)
                 wide(1)
                 offset(pair)
-                quant_dup(n - 1)
-                interleave(nc.scalar.copy, key, st["planes", n], mid, D)
+                if pair < 3:
+                    ff_copy(pair + 1, 1)
                 if pair == 0:
                     nc.scalar.copy(out=gain[:], in_=gain_bf[:].rearrange("p s t -> p (s t)"))
                     nc.scalar.copy(out=shift[:], in_=shift_bf[:].rearrange("p s t -> p (s t)"))
                 normalise(pair, 0)
                 normalise(pair, 1)
+                quant_dup(n - 1)
+                products()
                 wide(2)
                 wide(3)
-                if pair > 0:
-                    finish(2 * pair - 1)
-                if pair > 1:
-                    store(0 if pair == 2 else 4, 2 * pair)
-                interleave(nc.vector.tensor_copy, key, st["planes", n], 0, share)
             if part == 2:
+                if pair < 2:
+                    load_ff(2 * pair + 4)
+                    load_ff(2 * pair + 5)
                 h_turn(pair, 0)
                 h_turn(pair, 1)
-                interleave(nc.scalar.copy, key, st["planes", n], share, mid)
+                if pair < 3:
+                    ff_quant(pair + 1)
+                mix(nc.scalar.copy, share, mid)
                 affine(pair, 0)
                 affine(pair, 1)
                 if pair < 3:
-                    ff_turn(pair + 1, 0)
-                    ff_turn(pair + 1, 1)
-                interleave(nc.scalar.copy, key, st["planes", n], mid, D)
-                wide(0)
-                wide(1)
-                quant_dup(n - 1)
-                wide(2)
-                wide(3)
-                interleave(nc.vector.tensor_copy, key, st["planes", n], 0, share)
-            if part == 3:
-                if more:
-                    ff_copy(pair + 1, 0)
-                    ff_copy(pair + 1, 1)
-                interleave(nc.scalar.copy, key, st["planes", n], share, D)
-                h_group(pair)
-                wide(0)
-                h_quant(pair)
-                wide(1)
-                spread(2 * pair)
-                spread(2 * pair + 1)
-                if more:
-                    ff_quant(pair + 1)
-                second_product(n - 3)
-                second_product(n - 2)
-                if more:
                     for h in range(4):
                         first_product(pair + 1, h)
+                mix(nc.scalar.copy, mid, D)
+                wide(0)
+                wide(1)
                 quant_dup(n - 1)
-                second_product(n - 1)
+                products()
                 wide(2)
                 wide(3)
-                interleave(nc.vector.tensor_copy, key, st["planes", n], 0, share)
-                finish(2 * pair)
-        quant_dup(15)
-        second_product(15)
+            if n == 15:
+                interleave(nc.scalar.copy, key, st["planes", n], share // 2, 512)
+                interleave(nc.scalar.copy, key, st["planes", n], 512 + share // 2, D)
+            if part == 3:
+                if n < 15:
+                    mix(nc.scalar.copy, share, D)
+                wide(0)
+                if n == 14:
+                    h_quant(3)
+                wide(1)
+                wide(2)
+                wide(3)
+                quant_dup(n - 1)
+                products()
+            if n == 15:
+                interleave(nc.vector.tensor_copy, key, st["planes", n], 0, share // 2)
+                interleave(nc.vector.tensor_copy, key, st["planes", n], 512, 512 + share // 2)
+            else:
+                mix(nc.vector.tensor_copy, 0, share)
+            if part == 2:
+                h_group(pair)
+            for i in range(finished, closed):
+                finish(i)
+                if i in (3, 5):
+                    store(0 if i == 3 else 4, i + 1)
+            finished = closed
         finish(7)
         store(6, 8)

@@ -20,10 +20,11 @@ P = 128
 TILES = 8
 HEADS = 8
 ZROW = P + B
-HEAD_V = 384
-EDGE_V = 512
-W2_V = 512
-SHARES = (256, 512, 320, 160)
+HEAD_V = 320
+POOL_COLS = 352
+EDGE_V = 448
+W2_V = 496
+SHARES = (192, 544, 256, 96)
 
 
 def tile_mldecoder_pb_kernel(tc, ff_hid, tgt, w2, b2, g3, be3, dup_pool_bytes, dup_pool_scale, dup_bias, out):
@@ -32,6 +33,8 @@ def tile_mldecoder_pb_kernel(tc, ff_hid, tgt, w2, b2, g3, be3, dup_pool_bytes, d
     tgt_rows = tgt.rearrange("b k d -> (b k) d").rearrange("(p i) d -> i p d", i=TILES)
     w2_rows = w2.rearrange("(s p t) (hf n) -> hf s p t n", p=P, t=4, hf=2)
     dup_rows = dup_pool_bytes.rearrange("(j i) (s p t) g -> i s t p j g", i=TILES, s=2, t=4)
+
+    dup_wide = dup_pool_bytes.rearrange("(j i) (s p t) g -> i s p j (t g)", i=TILES, s=2, t=4)
 
     with ExitStack() as ctx:
         keep = ctx.enter_context(tc.tile_pool(name="keep", bufs=1))
@@ -58,7 +61,7 @@ def tile_mldecoder_pb_kernel(tc, ff_hid, tgt, w2, b2, g3, be3, dup_pool_bytes, d
 
         def load_dup(n):
             for t in range(4):
-                raw = work.tile([P, HEADS, G], U8, name="dup_raw", bufs=16)
+                raw = work.tile([P, HEADS, G], U8, name="dup_raw", bufs=12)
                 nc.sync.dma_start(out=raw[:], in_=dup_rows[n // 2, n % 2, t])
                 st["raw", n, t] = raw
 
@@ -87,6 +90,28 @@ def tile_mldecoder_pb_kernel(tc, ff_hid, tgt, w2, b2, g3, be3, dup_pool_bytes, d
         def widen_on_scalar(n, t):
             codes = st["raw", n, t][:].rearrange("p j g -> p (j g)").bitcast(FP8)
             nc.scalar.activation(out=st["planes", n][:, t, :], in_=codes, func=ACT.Copy, scale=dscale[:, n % 2, t : t + 1])
+
+        def load_rows(n):
+            for h in range(2):
+                raw = work.tile([P, 4, 4 * G], U8, name="dup_rows", bufs=4)
+                nc.sync.dma_start(out=raw[:], in_=dup_wide[n // 2, n % 2][:, 4 * h : 4 * h + 4])
+                st["rows", n, h] = raw
+
+        def widen_rows(n, on_scalar):
+            planes = work.tile([P, 4, HEADS * G], BF16, name="planes", bufs=6, align_bytes=64)
+            for j in range(HEADS):
+                for t in range(4):
+                    codes = st["rows", n, j // 4][:, j % 4, t * G : (t + 1) * G].bitcast(FP8)
+                    col = dscale[:, n % 2, t : t + 1]
+                    if j % 4 == 3 and on_scalar:
+                        nc.scalar.activation(out=planes[:, t, j * G : (j + 1) * G], in_=codes, func=ACT.Copy, scale=col)
+                    else:
+                        nc.vector.tensor_scalar(out=planes[:, t, j * G : (j + 1) * G], in0=codes, scalar1=col, scalar2=None, op0=ALU.mult)
+            st["planes", n] = planes
+
+        def interleave_on_gpsimd(key, planes, cols):
+            nc.gpsimd.tensor_scalar(out=st[key][:, :cols, :], in0=planes[:, :, :cols].rearrange("p t c -> p c t"),
+                                    scalar1=1.0, scalar2=0.0, op0=ALU.mult, op1=ALU.add)
 
         def new_grouped(key):
             st[key] = work.tile([P, 1024, 4], BF16, name="grouped", bufs=3, align_bytes=64)
@@ -265,9 +290,9 @@ def tile_mldecoder_pb_kernel(tc, ff_hid, tgt, w2, b2, g3, be3, dup_pool_bytes, d
         make_identity(nc, ident_b[:])
         for z in range(2):
             nc.vector.memset(zpad[z][:], 0)
-        load_dup(0)
+        load_rows(0)
         load_w2(0)
-        load_dup(1)
+        load_rows(1)
         load_w2(1)
         load_ff(0)
         load_ff(1)
@@ -284,6 +309,7 @@ def tile_mldecoder_pb_kernel(tc, ff_hid, tgt, w2, b2, g3, be3, dup_pool_bytes, d
         ff_turn(0, 1)
         load_ff(2)
         load_ff(3)
+        load_dup(4)
         b2_bank = psum.tile([P, P], BF16, name="bank", bufs=6)
         nc.tensor.transpose(b2_bank[:], b2_rows[:], ident_b[:])
 
@@ -295,16 +321,10 @@ def tile_mldecoder_pb_kernel(tc, ff_hid, tgt, w2, b2, g3, be3, dup_pool_bytes, d
         def quant_w2(s):
             quant(("w2g", s), w2_codes[s][:], w2_scales[s][:])
 
-        for t in range(4):
-            if t % 2 == 1:
-                widen_on_scalar(0, t)
-            else:
-                widen(0, t)
+        widen_rows(0, 3)
         both(("dup", 0), st["planes", 0], W2_V)
         both(("w2g", 0), st["w2", 0], W2_V)
-        for t in range(4):
-            widen(1, t)
-        load_dup(4)
+        widen_rows(1, 0)
         quant_dup(0)
         both(("dup", 1), st["planes", 1], HEAD_V)
         quant_w2(0)
@@ -388,8 +408,8 @@ def tile_mldecoder_pb_kernel(tc, ff_hid, tgt, w2, b2, g3, be3, dup_pool_bytes, d
                     quant_dup(n - 1)
                 products()
                 wide(2)
-                wide(3)
             if part == 1:
+                interleave_on_gpsimd(key, st["planes", n], POOL_COLS)
                 if pair < 3:
                     load_tgt(2 * pair + 2)
                     load_tgt(2 * pair + 3)
@@ -403,13 +423,13 @@ def tile_mldecoder_pb_kernel(tc, ff_hid, tgt, w2, b2, g3, be3, dup_pool_bytes, d
                 inverse(pair)
                 wide(1)
                 offset(pair)
-                if pair < 3:
-                    ff_copy(pair + 1, 1)
                 if pair == 0:
                     nc.scalar.copy(out=gain[:], in_=gain_bf[:].rearrange("p s t -> p (s t)"))
                     nc.scalar.copy(out=shift[:], in_=shift_bf[:].rearrange("p s t -> p (s t)"))
                 normalise(pair, 0)
                 normalise(pair, 1)
+                if pair < 3:
+                    ff_copy(pair + 1, 1)
                 quant_dup(n - 1)
                 products()
                 wide(2)
@@ -420,6 +440,8 @@ def tile_mldecoder_pb_kernel(tc, ff_hid, tgt, w2, b2, g3, be3, dup_pool_bytes, d
                     load_ff(2 * pair + 5)
                 h_turn(pair, 0)
                 h_turn(pair, 1)
+                wide(0)
+                wide(1)
                 if pair < 3:
                     ff_quant(pair + 1)
                 mix(nc.scalar.copy, share, mid)
@@ -429,8 +451,6 @@ def tile_mldecoder_pb_kernel(tc, ff_hid, tgt, w2, b2, g3, be3, dup_pool_bytes, d
                     for h in range(4):
                         first_product(pair + 1, h)
                 mix(nc.scalar.copy, mid, D)
-                wide(0)
-                wide(1)
                 quant_dup(n - 1)
                 products()
                 wide(2)
@@ -453,7 +473,7 @@ def tile_mldecoder_pb_kernel(tc, ff_hid, tgt, w2, b2, g3, be3, dup_pool_bytes, d
                 interleave(nc.vector.tensor_copy, key, st["planes", n], 0, share // 2)
                 interleave(nc.vector.tensor_copy, key, st["planes", n], 512, 512 + share // 2)
             else:
-                mix(nc.vector.tensor_copy, 0, share)
+                mix(nc.vector.tensor_copy, POOL_COLS if part == 1 else 0, share)
             if part == 2:
                 h_group(pair)
             for i in range(finished, closed):
@@ -461,5 +481,7 @@ def tile_mldecoder_pb_kernel(tc, ff_hid, tgt, w2, b2, g3, be3, dup_pool_bytes, d
                 if i in (3, 5):
                     store(0 if i == 3 else 4, i + 1)
             finished = closed
+            if part == 0:
+                wide(3)
         finish(7)
         store(6, 8)

from contextlib import ExitStack

import concourse.mybir as mybir
from concourse.masks import make_identity

B, K, G, D, FF = 16, 64, 128, 1024, 2048
EPS = 1e-5
FLOPS = 2 * B * K * FF * D + 2 * B * K * D * G

F32 = mybir.dt.float32
BF16 = mybir.dt.bfloat16
I32 = mybir.dt.int32
U8 = mybir.dt.uint8
FP8 = mybir.dt.float8_e4m3fn
FP8X4 = mybir.dt.float8_e4m3fn_x4
ALU = mybir.AluOpType
ACT = mybir.ActivationFunctionType

P = 128
TILES = 8
HEADS = 8
ZROW = P + B
HEAD_V = 320
POOL_COLS = 352
EDGE_V = 448
W2_V = 496
SHARES = (192, 544, 256, 96)


def tile_mldecoder_pb_kernel(tc, ff_hid, tgt, w2, b2, g3, be3, dup_pool_bytes, dup_pool_scale, dup_bias, out):
    nc = tc.nc
    ff_rows = ff_hid.rearrange("b k f -> (b k) f").rearrange("(p i) f -> i p f", i=TILES)
    tgt_rows = tgt.rearrange("b k d -> (b k) d").rearrange("(p i) d -> i p d", i=TILES)
    w2_rows = w2.rearrange("(s p t) (hf n) -> hf s p t n", p=P, t=4, hf=2)
    dup_rows = dup_pool_bytes.rearrange("(j i) (s p t) g -> i s t p j g", i=TILES, s=2, t=4)

    dup_wide = dup_pool_bytes.rearrange("(j i) (s p t) g -> i s p j (t g)", i=TILES, s=2, t=4)

    with ExitStack() as ctx:
        keep = ctx.enter_context(tc.tile_pool(name="keep", bufs=1))
        work = ctx.enter_context(tc.tile_pool(name="work", bufs=1))
        psum = ctx.enter_context(tc.psum_pool(name="psum", bufs=1))
        ctx.enter_context(tc.manual_schedule())

        dscale = keep.tile([P, 2, 4], F32, name="dscale")
        gain_bf = keep.tile([P, 2, 4], BF16, name="gain_bf")
        shift_bf = keep.tile([P, 2, 4], BF16, name="shift_bf")
        gain = keep.tile([P, 8], F32, name="gain")
        shift = keep.tile([P, 8], F32, name="shift")
        b2_rows = keep.tile([P, P], BF16, name="b2_rows")
        b2_col = keep.tile([P, 8], F32, name="b2_col")
        ident_f = keep.tile([P, P], F32, name="ident_f")
        ident_b = keep.tile([P, P], BF16, name="ident_b")
        obias = keep.tile([P, TILES, G], BF16, name="obias")
        osb = keep.tile([P, TILES, G], F32, name="osb")
        zpad = [keep.tile([P, 2, HEADS * ZROW], I32, name="zpad%d" % z, align_bytes=64) for z in range(2)]
        w2_codes = [keep.tile([P, D], I32, name="w2_codes%d" % s, align_bytes=64) for s in range(4)]
        w2_scales = [keep.tile([P, D], U8, name="w2_scales%d" % s, align_bytes=64) for s in range(4)]

        st = {}

        def load_dup(n):
            for t in range(4):
                raw = work.tile([P, HEADS, G], U8, name="dup_raw", bufs=12)
                nc.sync.dma_start(out=raw[:], in_=dup_rows[n // 2, n % 2, t])
                st["raw", n, t] = raw

        def load_w2(s):
            planes = work.tile([P, 4, D], BF16, name="planes", bufs=6, align_bytes=64)
            for ss in range(2):
                nc.sync.dma_start(out=planes[:, :, ss * 512 : (ss + 1) * 512], in_=w2_rows[s // 2, 2 * (s % 2) + ss])
            st["w2", s] = planes

        def load_ff(i):
            ffr = work.tile([P, FF], BF16, name="ff_raw", bufs=3)
            nc.sync.dma_start(out=ffr[:], in_=ff_rows[i])
            st["ff", i] = ffr

        def load_tgt(i):
            tg = work.tile([P, D], BF16, name="tgt_raw", bufs=4)
            nc.sync.dma_start(out=tg[:], in_=tgt_rows[i])
            st["tgt", i] = tg

        def widen(n, t):
            if t == 0:
                st["planes", n] = work.tile([P, 4, HEADS * G], BF16, name="planes", bufs=6, align_bytes=64)
            codes = st["raw", n, t][:].rearrange("p j g -> p (j g)").bitcast(FP8)
            nc.vector.tensor_scalar(out=st["planes", n][:, t, :], in0=codes, scalar1=dscale[:, n % 2, t : t + 1], scalar2=None, op0=ALU.mult)

        def widen_on_scalar(n, t):
            codes = st["raw", n, t][:].rearrange("p j g -> p (j g)").bitcast(FP8)
            nc.scalar.activation(out=st["planes", n][:, t, :], in_=codes, func=ACT.Copy, scale=dscale[:, n % 2, t : t + 1])

        def load_rows(n):
            for h in range(2):
                raw = work.tile([P, 4, 4 * G], U8, name="dup_rows", bufs=4)
                nc.sync.dma_start(out=raw[:], in_=dup_wide[n // 2, n % 2][:, 4 * h : 4 * h + 4])
                st["rows", n, h] = raw

        def widen_rows(n, on_scalar):
            planes = work.tile([P, 4, HEADS * G], BF16, name="planes", bufs=6, align_bytes=64)
            for j in range(HEADS):
                for t in range(4):
                    codes = st["rows", n, j // 4][:, j % 4, t * G : (t + 1) * G].bitcast(FP8)
                    col = dscale[:, n % 2, t : t + 1]
                    if j % 4 == 3 and on_scalar:
                        nc.scalar.activation(out=planes[:, t, j * G : (j + 1) * G], in_=codes, func=ACT.Copy, scale=col)
                    else:
                        nc.vector.tensor_scalar(out=planes[:, t, j * G : (j + 1) * G], in0=codes, scalar1=col, scalar2=None, op0=ALU.mult)
            st["planes", n] = planes

        def interleave_on_gpsimd(key, planes, cols):
            nc.gpsimd.tensor_scalar(out=st[key][:, :cols, :], in0=planes[:, :, :cols].rearrange("p t c -> p c t"),
                                    scalar1=1.0, scalar2=0.0, op0=ALU.mult, op1=ALU.add)

        def new_grouped(key):
            st[key] = work.tile([P, 1024, 4], BF16, name="grouped", bufs=3, align_bytes=64)

        def interleave(copy, key, planes, c0, c1):
            src = planes[:].rearrange("p t (c i) -> p c t i", i=4)
            dst = st[key][:].rearrange("p (c i) t -> p c t i", i=4)
            copy(out=dst[:, c0 // 4 : c1 // 4], in_=src[:, c0 // 4 : c1 // 4])

        def quant(key, codes, scales):
            nc.vector.quantize_mx(out=codes.bitcast(FP8X4), scales=scales, in_=st[key][:].rearrange("p c t -> p (c t)"))

        def quant_dup(n):
            codes = work.tile([P, HEADS * G], I32, name="dup_codes", bufs=6, align_bytes=64)
            scales = work.tile([P, HEADS * G], U8, name="dup_scales", bufs=6, align_bytes=64)
            flat = st["dup", n][:].rearrange("p c t -> p (c t)")
            parts = 2 if n == 15 else 1
            w = HEADS * G // parts
            for h in range(parts):
                nc.vector.quantize_mx(out=codes[:, h * w : (h + 1) * w].bitcast(FP8X4), scales=scales[:, h * w : (h + 1) * w],
                                      in_=flat[:, 4 * h * w : 4 * (h + 1) * w])
            st["dq", n] = (codes, scales)

        def ff_turn(pair, a):
            src = st["ff", 2 * pair + a][:].bitcast(F32)
            for h in range(2):
                bank = psum.tile([P, 2, 2, P], F32, name="bank", bufs=6)
                for s in range(2):
                    for u in range(2):
                        w0 = 256 * (2 * h + s)
                        nc.tensor.transpose(bank[:, s, u, :], src[:, w0 + u : w0 + 256 : 2], ident_f[:])
                st["ffb", pair, a, h] = bank

        def ff_copy(pair, a):
            words = st["ffg", pair][:].rearrange("p c t -> p (c t)").bitcast(F32).rearrange("p (s r u) -> p s r u", s=4, u=2)
            for h in range(2):
                nc.scalar.copy(out=words[:, 2 * h : 2 * h + 2, a * P : (a + 1) * P, :], in_=st["ffb", pair, a, h][:].rearrange("p s u r -> p s r u"))

        def ff_quant(pair):
            codes = work.tile([P, 1024], I32, name="ff_codes", bufs=2, align_bytes=64)
            scales = work.tile([P, 1024], U8, name="ff_scales", bufs=2, align_bytes=64)
            quant(("ffg", pair), codes[:], scales[:])
            st["ffq", pair] = (codes, scales)

        def first_product(pair, h):
            codes, scales = st["ffq", pair]
            bank = psum.tile([P, 2, 256], F32, name="bank", bufs=6)
            for q in range(2):
                c = 2 * h + q
                for s in range(4):
                    unit, c0 = 2 * (c // 4) + s // 2, (s % 2) * 512 + (c % 4) * P
                    nc.tensor.matmul_mx(
                        out=bank[:, q, :],
                        lhsT=w2_codes[unit][:, c0 : c0 + P].bitcast(FP8X4),
                        lhsT_scale=w2_scales[unit][:, c0 : c0 + P],
                        rhs=codes[:, s * 256 : (s + 1) * 256].bitcast(FP8X4),
                        rhs_scale=scales[:, s * 256 : (s + 1) * 256],
                        start=(s == 0), stop=(s == 3))
            st["mx1", pair, h] = bank

        def add_b2(pair, h):
            if h == 0:
                st["fft", pair] = work.tile([P, 8, 256], F32, name="fft", bufs=1)
            for q in range(2):
                c = 2 * h + q
                nc.scalar.activation(out=st["fft", pair][:, c, :], in_=st["mx1", pair, h][:, q, :], func=ACT.Identity, bias=b2_col[:, c : c + 1])

        def residual(pair, a, h):
            bank = psum.tile([P, 512], F32, name="bank", bufs=6)
            nc.tensor.matmul(bank[:], lhsT=ident_b[:], rhs=st["tgt", 2 * pair + a][:, h * 512 : (h + 1) * 512], start=True, stop=False)
            for q in range(4):
                nc.tensor.matmul(bank[:, q * P : (q + 1) * P], lhsT=st["fft", pair][:, 4 * h + q, a * P : (a + 1) * P], rhs=ident_f[:],
                                 is_transpose=True, start=False, stop=(q == 3))
            st["u", pair, a, h] = bank

        def moments(pair):
            stats = work.tile([P, 2, 2, 6], F32, name="stats", bufs=2)
            mean_var = work.tile([P, 2, 2], F32, name="mean_var", bufs=2)
            for a in range(2):
                for h in range(2):
                    nc.vector.bn_stats(out=stats[:, a, h, :], in_=st["u", pair, a, h][:])
            for a in range(2):
                nc.vector.bn_aggr(out=mean_var[:, a, :], in_=stats[:, a].rearrange("p h x -> p (h x)"))
            st["mv", pair] = mean_var

        def deviation(pair):
            std = work.tile([P, 2], F32, name="std", bufs=2)
            nc.scalar.activation(out=std[:], in_=st["mv", pair][:, :, 1], func=ACT.Sqrt, bias=EPS)
            st["std", pair] = std

        def inverse(pair):
            rstd = work.tile([P, 2], F32, name="rstd", bufs=2)
            nc.vector.reciprocal(out=rstd[:], in_=st["std", pair][:])
            st["rstd", pair] = rstd

        def offset(pair):
            nbias = work.tile([P, 2], F32, name="nbias", bufs=2)
            nc.vector.scalar_tensor_tensor(out=nbias[:], in0=st["mv", pair][:, :, 0], scalar=-1.0, in1=st["rstd", pair][:], op0=ALU.mult, op1=ALU.mult)
            st["nbias", pair] = nbias

        def normalise(pair, a):
            normed = work.tile([P, 2, 4, P], F32, name="normed", bufs=2)
            for h in range(2):
                nc.scalar.activation(out=normed[:, h], in_=st["u", pair, a, h][:].rearrange("r (p t) -> r t p", t=4), func=ACT.Identity,
                                     scale=st["rstd", pair][:, a : a + 1], bias=st["nbias", pair][:, a : a + 1])
            st["n", pair, a] = normed

        def h_turn(pair, s):
            for th in range(2):
                bank = psum.tile([P, 2, 2, P], F32, name="bank", bufs=6)
                for tt in range(2):
                    for a in range(2):
                        nc.tensor.transpose(bank[:, tt, a, :], st["n", pair, a][:, s, 2 * th + tt, :], ident_f[:])
                st["hb", pair, s, th] = bank

        def affine(pair, s):
            if s == 0:
                st["hp", pair] = work.tile([P, 2, 4, 256], BF16, name="hplanes", bufs=1, align_bytes=64)
            for t in range(4):
                nc.scalar.activation(
                    out=st["hp", pair][:, s, t, :].rearrange("p (a j b) -> p a j b", a=2, j=HEADS),
                    in_=st["hb", pair, s, t // 2][:, t % 2].rearrange("p a (b j) -> p a j b", j=HEADS),
                    func=ACT.Identity, scale=gain[:, 4 * s + t : 4 * s + t + 1], bias=shift[:, 4 * s + t : 4 * s + t + 1])

        def h_group(pair):
            hgrouped = work.tile([P, 512, 4], BF16, name="hgrouped", bufs=1, align_bytes=64)
            nc.vector.tensor_copy(
                out=hgrouped[:].rearrange("p (s c i) t -> p s c t i", s=2, i=4),
                in_=st["hp", pair][:].rearrange("p s t (c i) -> p s c t i", i=4))
            st["hg", pair] = hgrouped

        def h_quant(pair):
            codes = work.tile([P, 512], I32, name="h_codes", bufs=3, align_bytes=64)
            scales = work.tile([P, 512], U8, name="h_scales", bufs=3, align_bytes=64)
            quant(("hg", pair), codes[:], scales[:])
            st["hq", pair] = (codes, scales)

        def spread(i):
            codes = st["hq", i // 2][0]
            nc.vector.tensor_copy(
                out=zpad[i % 2][:].rearrange("p s (j x) -> p s j x", x=ZROW)[:, :, :, 0:B],
                in_=codes[:].rearrange("p (s a j b) -> p s a j b", s=2, a=2, b=B)[:, :, i % 2])

        def second_product(n):
            i, s = n // 2, n % 2
            if s == 0:
                st["o", i] = psum.tile([P, G], F32, name="out_bank", bufs=2)
            hscales = st["hq", i // 2][1]
            codes, scales = st["dq", n]
            c0 = s * 256 + (i % 2) * P
            for j in range(HEADS):
                nc.tensor.matmul_mx(
                    out=st["o", i][:],
                    lhsT=zpad[i % 2][:, s, j * P : (j + 1) * P].bitcast(FP8X4),
                    lhsT_scale=hscales[:, c0 : c0 + P],
                    rhs=codes[:, j * G : (j + 1) * G].bitcast(FP8X4),
                    rhs_scale=scales[:, j * G : (j + 1) * G],
                    start=(s == 0 and j == 0), stop=(s == 1 and j == HEADS - 1))

        def finish(i):
            nc.vector.tensor_tensor(out=osb[:, i, :], in0=st["o", i][:], in1=obias[:, i, :], op=ALU.add)

        def store(i0, i1):
            for j in range(HEADS):
                queue = nc.scalar if i1 == 8 and j % 2 else nc.sync
                queue.dma_start(
                    out=out[:, j * TILES * G + i0 * G : j * TILES * G + i1 * G],
                    in_=osb[j * B : (j + 1) * B, i0:i1, :].rearrange("p i g -> p (i g)"))

        nc.sync.dma_start(out=dscale[:], in_=dup_pool_scale.rearrange("o d z -> (o d z)").rearrange("(s p t) -> p s t", s=2, t=4))
        warm = keep.tile([P, 1], F32, name="warm")
        nc.vector.memset(warm[:], 1.0)
        nc.scalar.activation(out=warm[:], in_=warm[:], func=ACT.Sqrt)
        nc.gpsimd.memset(b2_rows[:], 0.0)
        make_identity(nc, ident_f[:])
        make_identity(nc, ident_b[:])
        for z in range(2):
            nc.vector.memset(zpad[z][:], 0)
        load_rows(0)
        load_w2(0)
        load_rows(1)
        load_w2(1)
        load_ff(0)
        load_ff(1)
        nc.sync.dma_start(out=b2_rows[0:8, :], in_=b2.rearrange("(c p) -> c p", p=P))
        load_w2(2)
        load_dup(2)
        load_w2(3)
        load_tgt(0)
        load_tgt(1)
        load_dup(3)
        nc.sync.dma_start(out=gain_bf[:], in_=g3.rearrange("(s p t) -> p s t", s=2, t=4))
        nc.sync.dma_start(out=shift_bf[:], in_=be3.rearrange("(s p t) -> p s t", s=2, t=4))
        ff_turn(0, 0)
        ff_turn(0, 1)
        load_ff(2)
        load_ff(3)
        load_dup(4)
        b2_bank = psum.tile([P, P], BF16, name="bank", bufs=6)
        nc.tensor.transpose(b2_bank[:], b2_rows[:], ident_b[:])

        def both(key, planes, share):
            new_grouped(key)
            interleave(nc.vector.tensor_copy, key, planes, 0, share)
            interleave(nc.scalar.copy, key, planes, share, D)

        def quant_w2(s):
            quant(("w2g", s), w2_codes[s][:], w2_scales[s][:])

        widen_rows(0, 3)
        both(("dup", 0), st["planes", 0], W2_V)
        both(("w2g", 0), st["w2", 0], W2_V)
        widen_rows(1, 0)
        quant_dup(0)
        both(("dup", 1), st["planes", 1], HEAD_V)
        quant_w2(0)
        both(("w2g", 1), st["w2", 1], W2_V)
        quant_dup(1)
        new_grouped(("ffg", 0))
        ff_copy(0, 0)
        ff_copy(0, 1)
        nc.scalar.copy(out=b2_col[:], in_=b2_bank[:, 0:8])
        quant_w2(1)
        both(("w2g", 2), st["w2", 2], W2_V)
        ff_quant(0)
        first_product(0, 0)
        first_product(0, 1)
        for t in range(4):
            widen(2, t)
        quant_w2(2)
        both(("w2g", 3), st["w2", 3], W2_V)
        add_b2(0, 0)
        add_b2(0, 1)
        quant_w2(3)
        first_product(0, 2)
        first_product(0, 3)

        multiplied = 0
        finished = 0
        for n in range(2, 17):
            pair, part = divmod(n - 2, 3)
            if pair > 3:
                part = 3
            share = SHARES[part] if n < 15 else EDGE_V
            mid = (share + D) // 64 * 32
            key = ("dup", n)

            def wide(t):
                if n < 15:
                    widen(n + 1, t)

            def mix(copy, c0, c1):
                if n < 16:
                    interleave(copy, key, st["planes", n], c0, c1)

            closed = multiplied // 2
            ready = [c for c in range(multiplied, n) if 3 * (c // 4) + 4 < n]
            multiplied += len(ready)

            def products():
                for c in ready:
                    if c % 2 == 0:
                        spread(c // 2)
                    second_product(c)

            if part == 1 and pair < 3:
                new_grouped(("ffg", pair + 1))
            if n < 16:
                new_grouped(key)
            if n + 3 < 16:
                load_dup(n + 3)
            if n == 2:
                for j in range(HEADS):
                    nc.sync.dma_start(out=obias[j * B : (j + 1) * B].rearrange("p i g -> p (i g)"),
                                      in_=dup_bias[j * TILES * G : (j + 1) * TILES * G].partition_broadcast(B))
            if part == 0:
                if pair > 0:
                    add_b2(pair, 0)
                    add_b2(pair, 1)
                mix(nc.scalar.copy, share, mid)
                add_b2(pair, 2)
                add_b2(pair, 3)
                mix(nc.scalar.copy, mid, D)
                for h in range(2):
                    for a in range(2):
                        residual(pair, a, h)
                if pair < 3:
                    ff_turn(pair + 1, 0)
                wide(0)
                if pair > 0:
                    h_quant(pair - 1)
                wide(1)
                if pair > 0:
                    quant_dup(n - 1)
                products()
                wide(2)
            if part == 1:
                interleave_on_gpsimd(key, st["planes", n], POOL_COLS)
                if pair < 3:
                    load_tgt(2 * pair + 2)
                    load_tgt(2 * pair + 3)
                    ff_copy(pair + 1, 0)
                    ff_turn(pair + 1, 1)
                moments(pair)
                mix(nc.scalar.copy, share, mid)
                deviation(pair)
                mix(nc.scalar.copy, mid, D)
                wide(0)
                inverse(pair)
                wide(1)
                offset(pair)
                if pair == 0:
                    nc.scalar.copy(out=gain[:], in_=gain_bf[:].rearrange("p s t -> p (s t)"))
                    nc.scalar.copy(out=shift[:], in_=shift_bf[:].rearrange("p s t -> p (s t)"))
                normalise(pair, 0)
                normalise(pair, 1)
                if pair < 3:
                    ff_copy(pair + 1, 1)
                quant_dup(n - 1)
                products()
                wide(2)
                wide(3)
            if part == 2:
                if pair < 2:
                    load_ff(2 * pair + 4)
                    load_ff(2 * pair + 5)
                h_turn(pair, 0)
                h_turn(pair, 1)
                wide(0)
                wide(1)
                if pair < 3:
                    ff_quant(pair + 1)
                mix(nc.scalar.copy, share, mid)
                affine(pair, 0)
                affine(pair, 1)
                if pair < 3:
                    for h in range(4):
                        first_product(pair + 1, h)
                mix(nc.scalar.copy, mid, D)
                quant_dup(n - 1)
                products()
                wide(2)
                wide(3)
            if n == 15:
                interleave(nc.scalar.copy, key, st["planes", n], share // 2, 512)
                interleave(nc.scalar.copy, key, st["planes", n], 512 + share // 2, D)
            if part == 3:
                if n < 15:
                    mix(nc.scalar.copy, share, D)
                wide(0)
                if n == 14:
                    h_quant(3)
                wide(1)
                wide(2)
                wide(3)
                quant_dup(n - 1)
                products()
            if n == 15:
                interleave(nc.vector.tensor_copy, key, st["planes", n], 0, share // 2)
                interleave(nc.vector.tensor_copy, key, st["planes", n], 512, 512 + share // 2)
            else:
                mix(nc.vector.tensor_copy, POOL_COLS if part == 1 else 0, share)
            if part == 2:
                h_group(pair)
            for i in range(finished, closed):
                finish(i)
                if i in (3, 5):
                    store(0 if i == 3 else 4, i + 1)
            finished = closed
            if part == 0:
                wide(3)
        finish(7)
        store(6, 8)
